import numpy as np
import ml_dtypes


def mxq(x, axis, fmt="e4m3"):
    dtype, down = {"e4m3": (ml_dtypes.float8_e4m3fn, 7), "e5m2": (ml_dtypes.float8_e5m2, 14)}[fmt]
    v = np.moveaxis(np.asarray(x, np.float32).astype(ml_dtypes.bfloat16).astype(np.float64), axis, -1)
    blocks = v.reshape(v.shape[:-1] + (-1, 32))
    amax = np.abs(blocks).max(-1, keepdims=True)
    byte = np.maximum(np.where(amax > 0, np.frexp(amax)[1] - 1 + 127, 0) - down, 1)
    scale = np.exp2(byte - 127.0)
    codes = (blocks / scale).astype(np.float32).astype(dtype).astype(np.float64)
    return np.moveaxis((codes * scale).reshape(v.shape), -1, axis)


WIDE = False


def mx_kscale(k):
    if not WIDE:
        return np.ones(k)
    levels = np.array([20, -20, 10, -10, 0])
    a = np.random.permutation(np.resize(levels, k // 512 * 4)).reshape(k // 512, 4)
    idx = np.arange(k)
    return np.exp2(a[idx // 512, idx % 128 // 32])


BF16 = ml_dtypes.bfloat16


def bf(x):
    return np.asarray(x, np.float32).astype(BF16)


def f64(x):
    return np.asarray(x).astype(np.float64)


B, L, C, K, D_MODEL, H, D_LLM = 2, 256, 16, 100, 128, 32, 128
D_KEYS = D_MODEL // H
G = H * D_KEYS
T = B * L


def setup_inputs():
    s = mx_kscale(T).reshape(B, L)
    attn_ctx = np.random.standard_normal((B, C, L, H, D_KEYS)) * 0.5 * s[:, None, :, None, None]
    Wo = np.random.standard_normal((C, H, D_KEYS, D_LLM)) * 2.0 / np.sqrt(G)
    bo = np.random.standard_normal((C, D_LLM)) * 0.5
    cluster_probs = np.random.uniform(size=(B, L, C))
    g = np.random.standard_normal((B, L, D_LLM)) * np.exp2(np.random.randint(-12, 1, (B, L, 1))) / s[:, :, None]
    return {
        "attn_ctx": bf(attn_ctx),
        "Wo": bf(Wo),
        "bo": bf(bo),
        "cluster_probs": bf(cluster_probs),
        "grad_out": bf(g),
    }


def reference(attn_ctx, Wo, bo, cluster_probs, grad_out):
    o = f64(attn_ctx).reshape(B, C, L, G).transpose(1, 0, 2, 3).reshape(C, T, G)
    p = f64(cluster_probs).reshape(T, C)
    g = f64(grad_out).reshape(T, D_LLM)
    gp = p.T[:, :, None] * g[None, :, :]
    dw = mxq(o, 1, "e4m3").transpose(0, 2, 1) @ mxq(gp, 1, "e5m2")
    return dw.reshape(C, H, D_KEYS, D_LLM)

@@ -1,0 +1,114 @@
+from contextlib import ExitStack
+
+import concourse.mybir as mybir
+
+BF16 = mybir.dt.bfloat16
+F32 = mybir.dt.float32
+U32 = mybir.dt.uint32
+U8 = mybir.dt.uint8
+E4M3_X4 = mybir.dt.float8_e4m3fn_x4
+E5M2_X4 = mybir.dt.float8_e5m2_x4
+
+P = 128
+PACK = 4
+B, C, L, G, E = 2, 16, 256, 128, 128
+GROUP = 4
+N_GROUPS = C // GROUP
+RUN = 4
+VECTOR_CLUSTERS = 1
+
+FLOPS = 2 * C * G * B * L * E
+BYTES = 2 * (B * C * L * G + B * L * C + B * L * E) + 4 * C * G * E
+
+
+def side_by_side(dst, src):
+    return (
+        dst.rearrange("p (w i) j -> p w j i", i=RUN),
+        src.rearrange("p j (w i) -> p w j i", i=RUN),
+    )
+
+
+def tile_model_pa_s_kernel(tc, attn_ctx, Wo, bo, cluster_probs, grad_out, out):
+    nc = tc.nc
+    with ExitStack() as ctx:
+        once = ctx.enter_context(tc.tile_pool(name="once", bufs=1))
+        per_group = ctx.enter_context(tc.tile_pool(name="per_group", bufs=N_GROUPS))
+        banks = ctx.enter_context(tc.psum_pool(name="banks", bufs=8))
+
+        probs_raw = once.tile([P, PACK, C], BF16)
+        grad_raw = once.tile([P, PACK, E], BF16)
+        for b in range(B):
+            nc.scalar.dma_start(
+                out=probs_raw[b:P:B], in_=cluster_probs[b].rearrange("(q j) c -> q j c", j=PACK)
+            )
+            nc.scalar.dma_start(
+                out=grad_raw[b:P:B], in_=grad_out[b].rearrange("(q j) e -> q j e", j=PACK)
+            )
+        ctx_raw = []
+        for n in range(N_GROUPS):
+            raw = per_group.tile([P, GROUP, PACK * G], BF16)
+            for b in range(B):
+                nc.sync.dma_start(
+                    out=raw[b:P:B],
+                    in_=attn_ctx[b, n * GROUP : (n + 1) * GROUP].rearrange(
+                        "c (q j) h d -> q c (j h d)", j=PACK
+                    ),
+                )
+            ctx_raw.append(raw)
+
+        probs_grouped = once.tile([P, C, PACK], BF16)
+        nc.vector.tensor_copy(out=probs_grouped[:], in_=probs_raw[:].rearrange("p j c -> p c j"))
+        grad_grouped = once.tile([P, E, PACK], BF16)
+        dst, src = side_by_side(grad_grouped[:], grad_raw[:])
+        nc.vector.tensor_copy(out=dst, in_=src)
+
+        for n in range(N_GROUPS):
+            clusters = slice(n * GROUP, (n + 1) * GROUP)
+
+            gp = per_group.tile([P, GROUP, E, PACK], BF16, align_bytes=64)
+            nc.vector.tensor_tensor(
+                out=gp[:],
+                in0=grad_grouped[:].unsqueeze(1).to_broadcast([P, GROUP, E, PACK]),
+                in1=probs_grouped[:, clusters, :].unsqueeze(2).to_broadcast([P, GROUP, E, PACK]),
+                op=mybir.AluOpType.mult,
+            )
+            gp_codes = per_group.tile([P, GROUP * E], U32, align_bytes=64)
+            gp_scales = per_group.tile([P, GROUP * E], U8, align_bytes=64)
+            nc.vector.quantize_mx(
+                out=gp_codes[:].bitcast(E5M2_X4),
+                scales=gp_scales[:],
+                in_=gp[:].rearrange("p c e j -> p (c e j)"),
+            )
+
+            ctx_grouped = per_group.tile([P, GROUP, G, PACK], BF16, align_bytes=64)
+            for i in range(GROUP):
+                dst, src = side_by_side(
+                    ctx_grouped[:, i], ctx_raw[n][:, i].rearrange("p (j g) -> p j g", j=PACK)
+                )
+                if i < GROUP - VECTOR_CLUSTERS:
+                    nc.scalar.copy(out=dst, in_=src)
+                else:
+                    nc.vector.tensor_copy(out=dst, in_=src)
+            ctx_codes = per_group.tile([P, GROUP * G], U32, align_bytes=64)
+            ctx_scales = per_group.tile([P, GROUP * G], U8, align_bytes=64)
+            nc.vector.quantize_mx(
+                out=ctx_codes[:].bitcast(E4M3_X4),
+                scales=ctx_scales[:],
+                in_=ctx_grouped[:].rearrange("p c g j -> p (c g j)"),
+            )
+
+            result = per_group.tile([P, GROUP, E], F32)
+            for i in range(GROUP):
+                own = slice(i * G, (i + 1) * G)
+                bank = banks.tile([P, GROUP * E], F32)
+                nc.tensor.matmul_mx(
+                    out=bank[:],
+                    lhsT=ctx_codes[:, own].bitcast(E4M3_X4),
+                    lhsT_scale=ctx_scales[:, own],
+                    rhs=gp_codes[:].bitcast(E5M2_X4),
+                    rhs_scale=gp_scales[:],
+                    start=True,
+                    stop=True,
+                )
+                nc.scalar.copy(out=result[:, i, :], in_=bank[:, own])
+            nc.sync.dma_start(out=out[clusters].rearrange("c h d e -> (h d) c e"), in_=result[:])

@@ -14,8 +14,11 @@ PACK = 4
 B, C, L, G, E = 2, 16, 256, 128, 128
 GROUP = 4
 N_GROUPS = C // GROUP
+LOAD = 2
 RUN = 4
-VECTOR_CLUSTERS = 1
+VECTOR_CLUSTERS = 3
+BANKS = 8
+LAG = 6
 
 FLOPS = 2 * C * G * B * L * E
 BYTES = 2 * (B * C * L * G + B * L * C + B * L * E) + 4 * C * G * E
@@ -32,25 +35,28 @@ def tile_model_pa_s_kernel(tc, attn_ctx, Wo, bo, cluster_probs, grad_out, out):
     nc = tc.nc
     with ExitStack() as ctx:
         once = ctx.enter_context(tc.tile_pool(name="once", bufs=1))
+        per_load = ctx.enter_context(tc.tile_pool(name="per_load", bufs=C // LOAD))
         per_group = ctx.enter_context(tc.tile_pool(name="per_group", bufs=N_GROUPS))
-        banks = ctx.enter_context(tc.psum_pool(name="banks", bufs=8))
+        per_cluster = ctx.enter_context(tc.tile_pool(name="per_cluster", bufs=C))
+        banks = ctx.enter_context(tc.psum_pool(name="banks", bufs=BANKS))
+        ctx.enter_context(tc.manual_schedule())
 
         probs_raw = once.tile([P, PACK, C], BF16)
         grad_raw = once.tile([P, PACK, E], BF16)
         for b in range(B):
-            nc.scalar.dma_start(
+            nc.sync.dma_start(
                 out=probs_raw[b:P:B], in_=cluster_probs[b].rearrange("(q j) c -> q j c", j=PACK)
             )
-            nc.scalar.dma_start(
+            nc.sync.dma_start(
                 out=grad_raw[b:P:B], in_=grad_out[b].rearrange("(q j) e -> q j e", j=PACK)
             )
         ctx_raw = []
-        for n in range(N_GROUPS):
-            raw = per_group.tile([P, GROUP, PACK * G], BF16)
+        for first in range(0, C, LOAD):
+            raw = per_load.tile([P, LOAD, PACK * G], BF16)
             for b in range(B):
                 nc.sync.dma_start(
                     out=raw[b:P:B],
-                    in_=attn_ctx[b, n * GROUP : (n + 1) * GROUP].rearrange(
+                    in_=attn_ctx[b, first : first + LOAD].rearrange(
                         "c (q j) h d -> q c (j h d)", j=PACK
                     ),
                 )
@@ -62,53 +68,88 @@ def tile_model_pa_s_kernel(tc, attn_ctx, Wo, bo, cluster_probs, grad_out, out):
         dst, src = side_by_side(grad_grouped[:], grad_raw[:])
         nc.vector.tensor_copy(out=dst, in_=src)
 
-        for n in range(N_GROUPS):
-            clusters = slice(n * GROUP, (n + 1) * GROUP)
+        gp_bf16, gp_codes, gp_scales = [], [], []
+        ctx_grouped, ctx_codes, ctx_scales, products_psum = [], [], [], []
 
+        def products(n):
             gp = per_group.tile([P, GROUP, E, PACK], BF16, align_bytes=64)
             nc.vector.tensor_tensor(
                 out=gp[:],
                 in0=grad_grouped[:].unsqueeze(1).to_broadcast([P, GROUP, E, PACK]),
-                in1=probs_grouped[:, clusters, :].unsqueeze(2).to_broadcast([P, GROUP, E, PACK]),
+                in1=probs_grouped[:, n * GROUP : (n + 1) * GROUP, :]
+                .unsqueeze(2)
+                .to_broadcast([P, GROUP, E, PACK]),
                 op=mybir.AluOpType.mult,
             )
-            gp_codes = per_group.tile([P, GROUP * E], U32, align_bytes=64)
-            gp_scales = per_group.tile([P, GROUP * E], U8, align_bytes=64)
-            nc.vector.quantize_mx(
-                out=gp_codes[:].bitcast(E5M2_X4),
-                scales=gp_scales[:],
-                in_=gp[:].rearrange("p c e j -> p (c e j)"),
-            )
+            gp_bf16.append(gp)
 
-            ctx_grouped = per_group.tile([P, GROUP, G, PACK], BF16, align_bytes=64)
-            for i in range(GROUP):
-                dst, src = side_by_side(
-                    ctx_grouped[:, i], ctx_raw[n][:, i].rearrange("p (j g) -> p j g", j=PACK)
-                )
-                if i < GROUP - VECTOR_CLUSTERS:
-                    nc.scalar.copy(out=dst, in_=src)
-                else:
-                    nc.vector.tensor_copy(out=dst, in_=src)
-            ctx_codes = per_group.tile([P, GROUP * G], U32, align_bytes=64)
-            ctx_scales = per_group.tile([P, GROUP * G], U8, align_bytes=64)
+        def quantise_gp(n):
+            codes = per_group.tile([P, GROUP * E], U32, align_bytes=64)
+            scales = per_group.tile([P, GROUP * E], U8, align_bytes=64)
             nc.vector.quantize_mx(
-                out=ctx_codes[:].bitcast(E4M3_X4),
-                scales=ctx_scales[:],
-                in_=ctx_grouped[:].rearrange("p c g j -> p (c g j)"),
+                out=codes[:].bitcast(E5M2_X4),
+                scales=scales[:],
+                in_=gp_bf16[n][:].rearrange("p c e j -> p (c e j)"),
             )
+            gp_codes.append(codes)
+            gp_scales.append(scales)
 
-            result = per_group.tile([P, GROUP, E], F32)
-            for i in range(GROUP):
-                own = slice(i * G, (i + 1) * G)
-                bank = banks.tile([P, GROUP * E], F32)
-                nc.tensor.matmul_mx(
-                    out=bank[:],
-                    lhsT=ctx_codes[:, own].bitcast(E4M3_X4),
-                    lhsT_scale=ctx_scales[:, own],
-                    rhs=gp_codes[:].bitcast(E5M2_X4),
-                    rhs_scale=gp_scales[:],
-                    start=True,
-                    stop=True,
-                )
-                nc.scalar.copy(out=result[:, i, :], in_=bank[:, own])
-            nc.sync.dma_start(out=out[clusters].rearrange("c h d e -> (h d) c e"), in_=result[:])
+        def regroup(c):
+            grouped = per_cluster.tile([P, G, PACK], BF16, align_bytes=64)
+            raw_c = ctx_raw[c // LOAD][:, c % LOAD].rearrange("p (j g) -> p j g", j=PACK)
+            dst_c, src_c = side_by_side(grouped[:], raw_c)
+            if c < C - VECTOR_CLUSTERS:
+                nc.scalar.copy(out=dst_c, in_=src_c)
+            else:
+                nc.vector.tensor_copy(out=dst_c, in_=src_c)
+            ctx_grouped.append(grouped)
+
+        def quantise_ctx(c):
+            codes_c = per_cluster.tile([P, G], U32, align_bytes=64)
+            scales_c = per_cluster.tile([P, G], U8, align_bytes=64)
+            nc.vector.quantize_mx(
+                out=codes_c[:].bitcast(E4M3_X4),
+                scales=scales_c[:],
+                in_=ctx_grouped[c][:].rearrange("p g j -> p (g j)"),
+            )
+            ctx_codes.append(codes_c)
+            ctx_scales.append(scales_c)
+
+        def multiply(c):
+            bank = banks.tile([P, GROUP * E], F32)
+            nc.tensor.matmul_mx(
+                out=bank[:],
+                lhsT=ctx_codes[c][:].bitcast(E4M3_X4),
+                lhsT_scale=ctx_scales[c][:],
+                rhs=gp_codes[c // GROUP][:].bitcast(E5M2_X4),
+                rhs_scale=gp_scales[c // GROUP][:],
+                start=True,
+                stop=True,
+            )
+            products_psum.append(bank)
+
+        def copy_out(c):
+            own = slice((c % GROUP) * E, (c % GROUP + 1) * E)
+            result = per_cluster.tile([P, E], F32)
+            nc.scalar.copy(out=result[:], in_=products_psum[c][:, own])
+            nc.sync.dma_start(out=out[c].rearrange("h d e -> (h d) e"), in_=result[:])
+
+        products(0)
+        products(1)
+        quantise_gp(0)
+        regroup(0)
+        for c in range(C):
+            if c + 1 < C:
+                regroup(c + 1)
+            quantise_ctx(c)
+            multiply(c)
+            if c >= LAG:
+                copy_out(c - LAG)
+            if c % GROUP == GROUP - 1:
+                n = c // GROUP
+                if n + 2 < N_GROUPS:
+                    products(n + 2)
+                if n + 1 < N_GROUPS:
+                    quantise_gp(n + 1)
+        for c in range(C - LAG, C):
+            copy_out(c)

@@ -1,6 +1,7 @@
 from contextlib import ExitStack
 
 import concourse.mybir as mybir
+from concourse.masks import make_identity
 
 BF16 = mybir.dt.bfloat16
 F32 = mybir.dt.float32
@@ -16,8 +17,7 @@ GROUP = 4
 N_GROUPS = C // GROUP
 LOAD = 2
 RUN = 4
-VECTOR_CLUSTERS = 3
-BANKS = 8
+BANKS = 7
 LAG = 6
 
 FLOPS = 2 * C * G * B * L * E
@@ -38,8 +38,13 @@ def tile_model_pa_s_kernel(tc, attn_ctx, Wo, bo, cluster_probs, grad_out, out):
         per_load = ctx.enter_context(tc.tile_pool(name="per_load", bufs=C // LOAD))
         per_group = ctx.enter_context(tc.tile_pool(name="per_group", bufs=N_GROUPS))
         per_cluster = ctx.enter_context(tc.tile_pool(name="per_cluster", bufs=C))
+        beside_products = ctx.enter_context(tc.tile_pool(name="beside_products", bufs=1))
         banks = ctx.enter_context(tc.psum_pool(name="banks", bufs=BANKS))
+        grad_bank = ctx.enter_context(tc.psum_pool(name="grad_bank", bufs=1))
         ctx.enter_context(tc.manual_schedule())
+
+        identity = once.tile([P, P], BF16)
+        make_identity(nc, identity[:])
 
         probs_raw = once.tile([P, PACK, C], BF16)
         grad_raw = once.tile([P, PACK, E], BF16)
@@ -67,15 +72,24 @@ def tile_model_pa_s_kernel(tc, attn_ctx, Wo, bo, cluster_probs, grad_out, out):
         grad_grouped = once.tile([P, E, PACK], BF16)
         dst, src = side_by_side(grad_grouped[:], grad_raw[:])
         nc.vector.tensor_copy(out=dst, in_=src)
+        grad_psum = grad_bank.tile([P, E, PACK], BF16)
+        nc.tensor.matmul(
+            out=grad_psum[:].rearrange("p e j -> p (e j)"),
+            lhsT=identity[:],
+            rhs=grad_grouped[:].rearrange("p e j -> p (e j)"),
+            start=True,
+            stop=True,
+        )
 
         gp_bf16, gp_codes, gp_scales = [], [], []
         ctx_grouped, ctx_codes, ctx_scales, products_psum = [], [], [], []
 
         def products(n):
             gp = per_group.tile([P, GROUP, E, PACK], BF16, align_bytes=64)
+            grad = grad_grouped if n == 0 else grad_psum
             nc.vector.tensor_tensor(
                 out=gp[:],
-                in0=grad_grouped[:].unsqueeze(1).to_broadcast([P, GROUP, E, PACK]),
+                in0=grad[:].unsqueeze(1).to_broadcast([P, GROUP, E, PACK]),
                 in1=probs_grouped[:, n * GROUP : (n + 1) * GROUP, :]
                 .unsqueeze(2)
                 .to_broadcast([P, GROUP, E, PACK]),
@@ -95,13 +109,24 @@ def tile_model_pa_s_kernel(tc, attn_ctx, Wo, bo, cluster_probs, grad_out, out):
             gp_scales.append(scales)
 
         def regroup(c):
-            grouped = per_cluster.tile([P, G, PACK], BF16, align_bytes=64)
             raw_c = ctx_raw[c // LOAD][:, c % LOAD].rearrange("p (j g) -> p j g", j=PACK)
-            dst_c, src_c = side_by_side(grouped[:], raw_c)
-            if c < C - VECTOR_CLUSTERS:
-                nc.scalar.copy(out=dst_c, in_=src_c)
+            if c % GROUP == GROUP - 1 and c < C - 1:
+                grouped = beside_products.tile([P, G, PACK], BF16, align_bytes=64)
+                nc.gpsimd.tensor_scalar(
+                    out=grouped[:],
+                    in0=raw_c.rearrange("p j g -> p g j"),
+                    scalar1=1.0,
+                    scalar2=0.0,
+                    op0=mybir.AluOpType.mult,
+                    op1=mybir.AluOpType.add,
+                )
             else:
-                nc.vector.tensor_copy(out=dst_c, in_=src_c)
+                grouped = per_cluster.tile([P, G, PACK], BF16, align_bytes=64)
+                dst_c, src_c = side_by_side(grouped[:], raw_c)
+                if c < C - 1:
+                    nc.scalar.copy(out=dst_c, in_=src_c)
+                else:
+                    nc.vector.tensor_copy(out=dst_c, in_=src_c)
             ctx_grouped.append(grouped)
 
         def quantise_ctx(c):

@@ -49,7 +49,7 @@ def tile_model_pa_s_kernel(tc, attn_ctx, Wo, bo, cluster_probs, grad_out, out):
         probs_raw = once.tile([P, PACK, C], BF16)
         grad_raw = once.tile([P, PACK, E], BF16)
         for b in range(B):
-            nc.sync.dma_start(
+            nc.scalar.dma_start(
                 out=probs_raw[b:P:B], in_=cluster_probs[b].rearrange("(q j) c -> q j c", j=PACK)
             )
             nc.sync.dma_start(

@@ -15,7 +15,7 @@ PACK = 4
 B, C, L, G, E = 2, 16, 256, 128, 128
 GROUP = 4
 N_GROUPS = C // GROUP
-LOAD = 2
+LOAD = 1
 RUN = 4
 BANKS = 7
 LAG = 6
@@ -48,23 +48,21 @@ def tile_model_pa_s_kernel(tc, attn_ctx, Wo, bo, cluster_probs, grad_out, out):
 
         probs_raw = once.tile([P, PACK, C], BF16)
         grad_raw = once.tile([P, PACK, E], BF16)
-        for b in range(B):
-            nc.scalar.dma_start(
-                out=probs_raw[b:P:B], in_=cluster_probs[b].rearrange("(q j) c -> q j c", j=PACK)
-            )
-            nc.sync.dma_start(
-                out=grad_raw[b:P:B], in_=grad_out[b].rearrange("(q j) e -> q j e", j=PACK)
-            )
+        nc.scalar.dma_start(
+            out=probs_raw[:].rearrange("p j c -> p (j c)"),
+            in_=cluster_probs.rearrange("b (q j) c -> q b (j c)", j=PACK),
+        )
+        nc.sync.dma_start(
+            out=grad_raw[:].rearrange("p j e -> p (j e)"),
+            in_=grad_out.rearrange("b (q j) e -> q b (j e)", j=PACK),
+        )
         ctx_raw = []
         for first in range(0, C, LOAD):
             raw = per_load.tile([P, LOAD, PACK * G], BF16)
-            for b in range(B):
-                nc.sync.dma_start(
-                    out=raw[b:P:B],
-                    in_=attn_ctx[b, first : first + LOAD].rearrange(
-                        "c (q j) h d -> q c (j h d)", j=PACK
-                    ),
-                )
+            nc.sync.dma_start(
+                out=raw[:].rearrange("p c x -> p (c x)"),
+                in_=attn_ctx[:, first].rearrange("b (q j) h d -> q b (j h d)", j=PACK),
+            )
             ctx_raw.append(raw)
 
         probs_grouped = once.tile([P, C, PACK], BF16)

@@ -40,7 +40,7 @@ def tile_model_pa_s_kernel(tc, attn_ctx, Wo, bo, cluster_probs, grad_out, out):
         per_cluster = ctx.enter_context(tc.tile_pool(name="per_cluster", bufs=C))
         beside_products = ctx.enter_context(tc.tile_pool(name="beside_products", bufs=1))
         banks = ctx.enter_context(tc.psum_pool(name="banks", bufs=BANKS))
-        grad_bank = ctx.enter_context(tc.psum_pool(name="grad_bank", bufs=1))
+        probs_bank = ctx.enter_context(tc.psum_pool(name="probs_bank", bufs=1))
         ctx.enter_context(tc.manual_schedule())
 
         identity = once.tile([P, P], BF16)
@@ -65,30 +65,27 @@ def tile_model_pa_s_kernel(tc, attn_ctx, Wo, bo, cluster_probs, grad_out, out):
             )
             ctx_raw.append(raw)
 
-        probs_grouped = once.tile([P, C, PACK], BF16)
-        nc.vector.tensor_copy(out=probs_grouped[:], in_=probs_raw[:].rearrange("p j c -> p c j"))
-        grad_grouped = once.tile([P, E, PACK], BF16)
-        dst, src = side_by_side(grad_grouped[:], grad_raw[:])
-        nc.vector.tensor_copy(out=dst, in_=src)
-        grad_psum = grad_bank.tile([P, E, PACK], BF16)
+        probs_psum = probs_bank.tile([P, C, PACK], BF16)
         nc.tensor.matmul(
-            out=grad_psum[:].rearrange("p e j -> p (e j)"),
+            out=probs_psum[:],
             lhsT=identity[:],
-            rhs=grad_grouped[:].rearrange("p e j -> p (e j)"),
+            rhs=probs_raw[:].rearrange("p j c -> p c j"),
             start=True,
             stop=True,
         )
+        grad_grouped = once.tile([P, E, PACK], BF16)
+        dst, src = side_by_side(grad_grouped[:], grad_raw[:])
+        nc.vector.tensor_copy(out=dst, in_=src)
 
         gp_bf16, gp_codes, gp_scales = [], [], []
         ctx_grouped, ctx_codes, ctx_scales, products_psum = [], [], [], []
 
         def products(n):
             gp = per_group.tile([P, GROUP, E, PACK], BF16, align_bytes=64)
-            grad = grad_grouped if n == 0 else grad_psum
             nc.vector.tensor_tensor(
                 out=gp[:],
-                in0=grad[:].unsqueeze(1).to_broadcast([P, GROUP, E, PACK]),
-                in1=probs_grouped[:, n * GROUP : (n + 1) * GROUP, :]
+                in0=grad_grouped[:].unsqueeze(1).to_broadcast([P, GROUP, E, PACK]),
+                in1=probs_psum[:, n * GROUP : (n + 1) * GROUP, :]
                 .unsqueeze(2)
                 .to_broadcast([P, GROUP, E, PACK]),
                 op=mybir.AluOpType.mult,

@@ -19,6 +19,7 @@ LOAD = 1
 RUN = 4
 BANKS = 7
 LAG = 6
+TURNED = 14
 
 FLOPS = 2 * C * G * B * L * E
 BYTES = 2 * (B * C * L * G + B * L * C + B * L * E) + 4 * C * G * E
@@ -40,7 +41,7 @@ def tile_model_pa_s_kernel(tc, attn_ctx, Wo, bo, cluster_probs, grad_out, out):
         per_cluster = ctx.enter_context(tc.tile_pool(name="per_cluster", bufs=C))
         beside_products = ctx.enter_context(tc.tile_pool(name="beside_products", bufs=1))
         banks = ctx.enter_context(tc.psum_pool(name="banks", bufs=BANKS))
-        probs_bank = ctx.enter_context(tc.psum_pool(name="probs_bank", bufs=1))
+        aside_bank = ctx.enter_context(tc.psum_pool(name="aside_bank", bufs=1))
         ctx.enter_context(tc.manual_schedule())
 
         identity = once.tile([P, P], BF16)
@@ -65,7 +66,8 @@ def tile_model_pa_s_kernel(tc, attn_ctx, Wo, bo, cluster_probs, grad_out, out):
             )
             ctx_raw.append(raw)
 
-        probs_psum = probs_bank.tile([P, C, PACK], BF16)
+        aside = aside_bank.tile([P, C, PACK], BF16)
+        probs_psum = aside
         nc.tensor.matmul(
             out=probs_psum[:],
             lhsT=identity[:],
@@ -78,7 +80,7 @@ def tile_model_pa_s_kernel(tc, attn_ctx, Wo, bo, cluster_probs, grad_out, out):
         nc.vector.tensor_copy(out=dst, in_=src)
 
         gp_bf16, gp_codes, gp_scales = [], [], []
-        ctx_grouped, ctx_codes, ctx_scales, products_psum = [], [], [], []
+        ctx_grouped, ctx_codes, ctx_scales, products_psum, turned_psum = [], [], [], [], []
 
         def products(n):
             gp = per_group.tile([P, GROUP, E, PACK], BF16, align_bytes=64)
@@ -115,6 +117,9 @@ def tile_model_pa_s_kernel(tc, attn_ctx, Wo, bo, cluster_probs, grad_out, out):
                     op0=mybir.AluOpType.mult,
                     op1=mybir.AluOpType.add,
                 )
+            elif c == TURNED:
+                grouped = per_cluster.tile([P, G, PACK], BF16, align_bytes=64)
+                nc.scalar.copy(out=grouped[:], in_=turned_psum[0][:])
             else:
                 grouped = per_cluster.tile([P, G, PACK], BF16, align_bytes=64)
                 dst_c, src_c = side_by_side(grouped[:], raw_c)
@@ -123,6 +128,12 @@ def tile_model_pa_s_kernel(tc, attn_ctx, Wo, bo, cluster_probs, grad_out, out):
                 else:
                     nc.vector.tensor_copy(out=dst_c, in_=src_c)
             ctx_grouped.append(grouped)
+
+        def turn(c):
+            raw_c = ctx_raw[c // LOAD][:, c % LOAD].rearrange("p (j g) -> p g j", j=PACK)
+            aside = aside_bank.tile([P, G, PACK], BF16)
+            nc.tensor.matmul(out=aside[:], lhsT=identity[:], rhs=raw_c, start=True, stop=True)
+            turned_psum.append(aside)
 
         def quantise_ctx(c):
             codes_c = per_cluster.tile([P, G], U32, align_bytes=64)
@@ -169,6 +180,8 @@ def tile_model_pa_s_kernel(tc, attn_ctx, Wo, bo, cluster_probs, grad_out, out):
                 n = c // GROUP
                 if n + 2 < N_GROUPS:
                     products(n + 2)
+                if n + 2 == N_GROUPS - 1:
+                    turn(TURNED)
                 if n + 1 < N_GROUPS:
                     quantise_gp(n + 1)
         for c in range(C - LAG, C):

@@ -15,6 +15,7 @@ PACK = 4
 B, C, L, G, E = 2, 16, 256, 128, 128
 GROUP = 4
 N_GROUPS = C // GROUP
+PAIR = 2
 LOAD = 1
 RUN = 4
 BANKS = 7
@@ -37,7 +38,6 @@ def tile_model_pa_s_kernel(tc, attn_ctx, Wo, bo, cluster_probs, grad_out, out):
     with ExitStack() as ctx:
         once = ctx.enter_context(tc.tile_pool(name="once", bufs=1))
         per_load = ctx.enter_context(tc.tile_pool(name="per_load", bufs=C // LOAD))
-        per_group = ctx.enter_context(tc.tile_pool(name="per_group", bufs=N_GROUPS))
         per_cluster = ctx.enter_context(tc.tile_pool(name="per_cluster", bufs=C))
         beside_products = ctx.enter_context(tc.tile_pool(name="beside_products", bufs=1))
         banks = ctx.enter_context(tc.psum_pool(name="banks", bufs=BANKS))
@@ -79,31 +79,29 @@ def tile_model_pa_s_kernel(tc, attn_ctx, Wo, bo, cluster_probs, grad_out, out):
         dst, src = side_by_side(grad_grouped[:], grad_raw[:])
         nc.vector.tensor_copy(out=dst, in_=src)
 
-        gp_bf16, gp_codes, gp_scales = [], [], []
+        gp_bf16 = once.tile([P, C, E, PACK], BF16, align_bytes=64)
+        gp_codes = once.tile([P, C * E], U32, align_bytes=64)
+        gp_scales = once.tile([P, C * E], U8, align_bytes=64)
         ctx_grouped, ctx_codes, ctx_scales, products_psum, turned_psum = [], [], [], [], []
 
         def products(n):
-            gp = per_group.tile([P, GROUP, E, PACK], BF16, align_bytes=64)
+            group = slice(n * GROUP, (n + 1) * GROUP)
             nc.vector.tensor_tensor(
-                out=gp[:],
+                out=gp_bf16[:, group],
                 in0=grad_grouped[:].unsqueeze(1).to_broadcast([P, GROUP, E, PACK]),
-                in1=probs_psum[:, n * GROUP : (n + 1) * GROUP, :]
-                .unsqueeze(2)
-                .to_broadcast([P, GROUP, E, PACK]),
+                in1=probs_psum[:, group, :].unsqueeze(2).to_broadcast([P, GROUP, E, PACK]),
                 op=mybir.AluOpType.mult,
             )
-            gp_bf16.append(gp)
 
-        def quantise_gp(n):
-            codes = per_group.tile([P, GROUP * E], U32, align_bytes=64)
-            scales = per_group.tile([P, GROUP * E], U8, align_bytes=64)
+        def quantise_gp(first, end):
             nc.vector.quantize_mx(
-                out=codes[:].bitcast(E5M2_X4),
-                scales=scales[:],
-                in_=gp_bf16[n][:].rearrange("p c e j -> p (c e j)"),
+                out=gp_codes[:, first * E : end * E].bitcast(E5M2_X4),
+                scales=gp_scales[:, first * E : end * E],
+                in_=gp_bf16[:, first:end].rearrange("p c e j -> p (c e j)"),
             )
-            gp_codes.append(codes)
-            gp_scales.append(scales)
+
+        def window_start(c):
+            return max(0, (c // PAIR + 1) * PAIR - GROUP)
 
         def regroup(c):
             raw_c = ctx_raw[c // LOAD][:, c % LOAD].rearrange("p (j g) -> p j g", j=PACK)
@@ -123,10 +121,7 @@ def tile_model_pa_s_kernel(tc, attn_ctx, Wo, bo, cluster_probs, grad_out, out):
             else:
                 grouped = per_cluster.tile([P, G, PACK], BF16, align_bytes=64)
                 dst_c, src_c = side_by_side(grouped[:], raw_c)
-                if c < C - 1:
-                    nc.scalar.copy(out=dst_c, in_=src_c)
-                else:
-                    nc.vector.tensor_copy(out=dst_c, in_=src_c)
+                nc.scalar.copy(out=dst_c, in_=src_c)
             ctx_grouped.append(grouped)
 
         def turn(c):
@@ -148,30 +143,36 @@ def tile_model_pa_s_kernel(tc, attn_ctx, Wo, bo, cluster_probs, grad_out, out):
 
         def multiply(c):
             bank = banks.tile([P, GROUP * E], F32)
+            columns = slice(window_start(c) * E, (window_start(c) + GROUP) * E)
             nc.tensor.matmul_mx(
                 out=bank[:],
                 lhsT=ctx_codes[c][:].bitcast(E4M3_X4),
                 lhsT_scale=ctx_scales[c][:],
-                rhs=gp_codes[c // GROUP][:].bitcast(E5M2_X4),
-                rhs_scale=gp_scales[c // GROUP][:],
+                rhs=gp_codes[:, columns].bitcast(E5M2_X4),
+                rhs_scale=gp_scales[:, columns],
                 start=True,
                 stop=True,
             )
             products_psum.append(bank)
 
-        def copy_out(c):
-            own = slice((c % GROUP) * E, (c % GROUP + 1) * E)
+        def copy_out(c, on_vector=False):
+            own = slice((c - window_start(c)) * E, (c - window_start(c) + 1) * E)
             result = per_cluster.tile([P, E], F32)
-            nc.scalar.copy(out=result[:], in_=products_psum[c][:, own])
+            if on_vector:
+                nc.vector.tensor_copy(out=result[:], in_=products_psum[c][:, own])
+            else:
+                nc.scalar.copy(out=result[:], in_=products_psum[c][:, own])
             nc.sync.dma_start(out=out[c].rearrange("h d e -> (h d) e"), in_=result[:])
 
         products(0)
         products(1)
-        quantise_gp(0)
+        quantise_gp(0, GROUP)
         regroup(0)
         for c in range(C):
             if c + 1 < C:
                 regroup(c + 1)
+            if c >= GROUP and c % PAIR == 0:
+                quantise_gp(c, c + PAIR)
             quantise_ctx(c)
             multiply(c)
             if c >= LAG:
@@ -182,7 +183,5 @@ def tile_model_pa_s_kernel(tc, attn_ctx, Wo, bo, cluster_probs, grad_out, out):
                     products(n + 2)
                 if n + 2 == N_GROUPS - 1:
                     turn(TURNED)
-                if n + 1 < N_GROUPS:
-                    quantise_gp(n + 1)
         for c in range(C - LAG, C):
-            copy_out(c)
+            copy_out(c, on_vector=(C - 1 - c) % 2 == 1)

@@ -16,6 +16,7 @@ B, C, L, G, E = 2, 16, 256, 128, 128
 GROUP = 4
 N_GROUPS = C // GROUP
 PAIR = 2
+STORE = 2
 LOAD = 1
 RUN = 4
 BANKS = 7
@@ -82,7 +83,7 @@ def tile_model_pa_s_kernel(tc, attn_ctx, Wo, bo, cluster_probs, grad_out, out):
         gp_bf16 = once.tile([P, C, E, PACK], BF16, align_bytes=64)
         gp_codes = once.tile([P, C * E], U32, align_bytes=64)
         gp_scales = once.tile([P, C * E], U8, align_bytes=64)
-        ctx_grouped, ctx_codes, ctx_scales, products_psum, turned_psum = [], [], [], [], []
+        ctx_grouped, ctx_codes, ctx_scales, products_psum, turned_psum, results = [], [], [], [], [], []
 
         def products(n):
             group = slice(n * GROUP, (n + 1) * GROUP)
@@ -157,12 +158,19 @@ def tile_model_pa_s_kernel(tc, attn_ctx, Wo, bo, cluster_probs, grad_out, out):
 
         def copy_out(c, on_vector=False):
             own = slice((c - window_start(c)) * E, (c - window_start(c) + 1) * E)
-            result = per_cluster.tile([P, E], F32)
+            together = STORE if c < C - GROUP else 1
+            if c % together == 0:
+                result = per_cluster.tile([P, together, E], F32)
+                results.append(result)
             if on_vector:
-                nc.vector.tensor_copy(out=result[:], in_=products_psum[c][:, own])
+                nc.vector.tensor_copy(out=results[-1][:, c % together], in_=products_psum[c][:, own])
             else:
-                nc.scalar.copy(out=result[:], in_=products_psum[c][:, own])
-            nc.sync.dma_start(out=out[c].rearrange("h d e -> (h d) e"), in_=result[:])
+                nc.scalar.copy(out=results[-1][:, c % together], in_=products_psum[c][:, own])
+            if c % together == together - 1:
+                nc.sync.dma_start(
+                    out=out[c + 1 - together : c + 1].rearrange("c h d e -> (h d) c e"),
+                    in_=results[-1][:],
+                )
 
         products(0)
         products(1)

@@ -23,6 +23,8 @@ BANKS = 7
 LAG = 6
 TURNED = 14
 
+HALVES = tuple(slice(i * E // 4, (i + 1) * E // 4) for i in range(4))
+
 FLOPS = 2 * C * G * B * L * E
 BYTES = 2 * (B * C * L * G + B * L * C + B * L * E) + 4 * C * G * E
 
@@ -77,20 +79,22 @@ def tile_model_pa_s_kernel(tc, attn_ctx, Wo, bo, cluster_probs, grad_out, out):
             stop=True,
         )
         grad_grouped = once.tile([P, E, PACK], BF16)
-        dst, src = side_by_side(grad_grouped[:], grad_raw[:])
-        nc.vector.tensor_copy(out=dst, in_=src)
+        for half in HALVES:
+            dst, src = side_by_side(grad_grouped[:, half, :], grad_raw[:, :, half])
+            nc.vector.tensor_copy(out=dst, in_=src)
 
         gp_bf16 = once.tile([P, C, E, PACK], BF16, align_bytes=64)
         gp_codes = once.tile([P, C * E], U32, align_bytes=64)
         gp_scales = once.tile([P, C * E], U8, align_bytes=64)
         ctx_grouped, ctx_codes, ctx_scales, products_psum, turned_psum, results = [], [], [], [], [], []
 
-        def products(n):
+        def products(n, columns=slice(0, E)):
             group = slice(n * GROUP, (n + 1) * GROUP)
+            shape = [P, GROUP, columns.stop - columns.start, PACK]
             nc.vector.tensor_tensor(
-                out=gp_bf16[:, group],
-                in0=grad_grouped[:].unsqueeze(1).to_broadcast([P, GROUP, E, PACK]),
-                in1=probs_psum[:, group, :].unsqueeze(2).to_broadcast([P, GROUP, E, PACK]),
+                out=gp_bf16[:, group, columns, :],
+                in0=grad_grouped[:, columns, :].unsqueeze(1).to_broadcast(shape),
+                in1=probs_psum[:, group, :].unsqueeze(2).to_broadcast(shape),
                 op=mybir.AluOpType.mult,
             )
 
@@ -172,7 +176,8 @@ def tile_model_pa_s_kernel(tc, attn_ctx, Wo, bo, cluster_probs, grad_out, out):
                     in_=results[-1][:],
                 )
 
-        products(0)
+        for half in HALVES:
+            products(0, half)
         products(1)
         quantise_gp(0, GROUP)
         regroup(0)

from contextlib import ExitStack

import concourse.mybir as mybir
from concourse.masks import make_identity

BF16 = mybir.dt.bfloat16
F32 = mybir.dt.float32
U32 = mybir.dt.uint32
U8 = mybir.dt.uint8
E4M3_X4 = mybir.dt.float8_e4m3fn_x4
E5M2_X4 = mybir.dt.float8_e5m2_x4

P = 128
PACK = 4
B, C, L, G, E = 2, 16, 256, 128, 128
GROUP = 4
N_GROUPS = C // GROUP
PAIR = 2
STORE = 2
LOAD = 1
RUN = 4
BANKS = 7
LAG = 6
TURNED = 14

HALVES = tuple(slice(i * E // 4, (i + 1) * E // 4) for i in range(4))

FLOPS = 2 * C * G * B * L * E
BYTES = 2 * (B * C * L * G + B * L * C + B * L * E) + 4 * C * G * E


def side_by_side(dst, src):
    return (
        dst.rearrange("p (w i) j -> p w j i", i=RUN),
        src.rearrange("p j (w i) -> p w j i", i=RUN),
    )


def tile_model_pa_s_kernel(tc, attn_ctx, Wo, bo, cluster_probs, grad_out, out):
    nc = tc.nc
    with ExitStack() as ctx:
        once = ctx.enter_context(tc.tile_pool(name="once", bufs=1))
        per_load = ctx.enter_context(tc.tile_pool(name="per_load", bufs=C // LOAD))
        per_cluster = ctx.enter_context(tc.tile_pool(name="per_cluster", bufs=C))
        beside_products = ctx.enter_context(tc.tile_pool(name="beside_products", bufs=1))
        banks = ctx.enter_context(tc.psum_pool(name="banks", bufs=BANKS))
        aside_bank = ctx.enter_context(tc.psum_pool(name="aside_bank", bufs=1))
        ctx.enter_context(tc.manual_schedule())

        identity = once.tile([P, P], BF16)
        make_identity(nc, identity[:])

        probs_raw = once.tile([P, PACK, C], BF16)
        grad_raw = once.tile([P, PACK, E], BF16)
        nc.scalar.dma_start(
            out=probs_raw[:].rearrange("p j c -> p (j c)"),
            in_=cluster_probs.rearrange("b (q j) c -> q b (j c)", j=PACK),
        )
        nc.sync.dma_start(
            out=grad_raw[:].rearrange("p j e -> p (j e)"),
            in_=grad_out.rearrange("b (q j) e -> q b (j e)", j=PACK),
        )
        ctx_raw = []
        for first in range(0, C, LOAD):
            raw = per_load.tile([P, LOAD, PACK * G], BF16)
            nc.sync.dma_start(
                out=raw[:].rearrange("p c x -> p (c x)"),
                in_=attn_ctx[:, first].rearrange("b (q j) h d -> q b (j h d)", j=PACK),
            )
            ctx_raw.append(raw)

        aside = aside_bank.tile([P, C, PACK], BF16)
        probs_psum = aside
        nc.tensor.matmul(
            out=probs_psum[:],
            lhsT=identity[:],
            rhs=probs_raw[:].rearrange("p j c -> p c j"),
            start=True,
            stop=True,
        )
        grad_grouped = once.tile([P, E, PACK], BF16)
        for half in HALVES:
            dst, src = side_by_side(grad_grouped[:, half, :], grad_raw[:, :, half])
            nc.vector.tensor_copy(out=dst, in_=src)

        gp_bf16 = once.tile([P, C, E, PACK], BF16, align_bytes=64)
        gp_codes = once.tile([P, C * E], U32, align_bytes=64)
        gp_scales = once.tile([P, C * E], U8, align_bytes=64)
        ctx_grouped, ctx_codes, ctx_scales, products_psum, turned_psum, results = [], [], [], [], [], []

        def products(n, columns=slice(0, E)):
            group = slice(n * GROUP, (n + 1) * GROUP)
            shape = [P, GROUP, columns.stop - columns.start, PACK]
            nc.vector.tensor_tensor(
                out=gp_bf16[:, group, columns, :],
                in0=grad_grouped[:, columns, :].unsqueeze(1).to_broadcast(shape),
                in1=probs_psum[:, group, :].unsqueeze(2).to_broadcast(shape),
                op=mybir.AluOpType.mult,
            )

        def quantise_gp(first, end):
            nc.vector.quantize_mx(
                out=gp_codes[:, first * E : end * E].bitcast(E5M2_X4),
                scales=gp_scales[:, first * E : end * E],
                in_=gp_bf16[:, first:end].rearrange("p c e j -> p (c e j)"),
            )

        def window_start(c):
            return max(0, (c // PAIR + 1) * PAIR - GROUP)

        def regroup(c):
            raw_c = ctx_raw[c // LOAD][:, c % LOAD].rearrange("p (j g) -> p j g", j=PACK)
            if c % GROUP == GROUP - 1 and c < C - 1:
                grouped = beside_products.tile([P, G, PACK], BF16, align_bytes=64)
                nc.gpsimd.tensor_scalar(
                    out=grouped[:],
                    in0=raw_c.rearrange("p j g -> p g j"),
                    scalar1=1.0,
                    scalar2=0.0,
                    op0=mybir.AluOpType.mult,
                    op1=mybir.AluOpType.add,
                )
            elif c == TURNED:
                grouped = per_cluster.tile([P, G, PACK], BF16, align_bytes=64)
                nc.scalar.copy(out=grouped[:], in_=turned_psum[0][:])
            else:
                grouped = per_cluster.tile([P, G, PACK], BF16, align_bytes=64)
                dst_c, src_c = side_by_side(grouped[:], raw_c)
                nc.scalar.copy(out=dst_c, in_=src_c)
            ctx_grouped.append(grouped)

        def turn(c):
            raw_c = ctx_raw[c // LOAD][:, c % LOAD].rearrange("p (j g) -> p g j", j=PACK)
            aside = aside_bank.tile([P, G, PACK], BF16)
            nc.tensor.matmul(out=aside[:], lhsT=identity[:], rhs=raw_c, start=True, stop=True)
            turned_psum.append(aside)

        def quantise_ctx(c):
            codes_c = per_cluster.tile([P, G], U32, align_bytes=64)
            scales_c = per_cluster.tile([P, G], U8, align_bytes=64)
            nc.vector.quantize_mx(
                out=codes_c[:].bitcast(E4M3_X4),
                scales=scales_c[:],
                in_=ctx_grouped[c][:].rearrange("p g j -> p (g j)"),
            )
            ctx_codes.append(codes_c)
            ctx_scales.append(scales_c)

        def multiply(c):
            bank = banks.tile([P, GROUP * E], F32)
            columns = slice(window_start(c) * E, (window_start(c) + GROUP) * E)
            nc.tensor.matmul_mx(
                out=bank[:],
                lhsT=ctx_codes[c][:].bitcast(E4M3_X4),
                lhsT_scale=ctx_scales[c][:],
                rhs=gp_codes[:, columns].bitcast(E5M2_X4),
                rhs_scale=gp_scales[:, columns],
                start=True,
                stop=True,
            )
            products_psum.append(bank)

        def copy_out(c, on_vector=False):
            own = slice((c - window_start(c)) * E, (c - window_start(c) + 1) * E)
            together = STORE if c < C - GROUP else 1
            if c % together == 0:
                result = per_cluster.tile([P, together, E], F32)
                results.append(result)
            if on_vector:
                nc.vector.tensor_copy(out=results[-1][:, c % together], in_=products_psum[c][:, own])
            else:
                nc.scalar.copy(out=results[-1][:, c % together], in_=products_psum[c][:, own])
            if c % together == together - 1:
                nc.sync.dma_start(
                    out=out[c + 1 - together : c + 1].rearrange("c h d e -> (h d) c e"),
                    in_=results[-1][:],
                )

        for half in HALVES:
            products(0, half)
        products(1)
        quantise_gp(0, GROUP)
        regroup(0)
        for c in range(C):
            if c + 1 < C:
                regroup(c + 1)
            if c >= GROUP and c % PAIR == 0:
                quantise_gp(c, c + PAIR)
            quantise_ctx(c)
            multiply(c)
            if c >= LAG:
                copy_out(c - LAG)
            if c % GROUP == GROUP - 1:
                n = c // GROUP
                if n + 2 < N_GROUPS:
                    products(n + 2)
                if n + 2 == N_GROUPS - 1:
                    turn(TURNED)
        for c in range(C - LAG, C):
            copy_out(c, on_vector=(C - 1 - c) % 2 == 1)
